import numpy as np
import ml_dtypes


def mxq(x, axis, fmt="e4m3"):
    dtype, down = {"e4m3": (ml_dtypes.float8_e4m3fn, 7), "e5m2": (ml_dtypes.float8_e5m2, 14)}[fmt]
    v = np.moveaxis(np.asarray(x, np.float32).astype(ml_dtypes.bfloat16).astype(np.float64), axis, -1)
    blocks = v.reshape(v.shape[:-1] + (-1, 32))
    amax = np.abs(blocks).max(-1, keepdims=True)
    byte = np.maximum(np.where(amax > 0, np.frexp(amax)[1] - 1 + 127, 0) - down, 1)
    scale = np.exp2(byte - 127.0)
    codes = (blocks / scale).astype(np.float32).astype(dtype).astype(np.float64)
    return np.moveaxis((codes * scale).reshape(v.shape), -1, axis)


WIDE = False


def mx_kscale(k):
    if not WIDE:
        return np.ones(k)
    levels = np.array([18, -18])
    if k % 512:
        return np.exp2(np.random.permutation(np.resize(levels, k // 32))).repeat(32)
    a = np.empty((k // 512, 16))
    for p in range(k // 512):
        a[p, :8] = np.random.permutation(np.resize(levels, 8))
        for g in range(8):
            far = levels[np.abs(levels - a[p, g]) >= 10]
            a[p, g + 8] = far[np.random.randint(len(far))]
    return np.exp2(a.ravel()).repeat(32)


BF16 = ml_dtypes.bfloat16


def bf(x):
    return np.asarray(x, np.float32).astype(BF16)


def f64(x):
    return np.asarray(x).astype(np.float64)


B, T, C, NH, NKV, HD = 1, 512, 1536, 16, 4, 128
JQ, JK = NH * HD, NKV * HD


def rope(u, angles):
    up = u.reshape(u.shape[:-1] + (HD // 2, 2))
    cos = np.cos(angles)[None, :, None, :]
    sin = np.sin(angles)[None, :, None, :]
    u0, u1 = up[..., 0], up[..., 1]
    return np.stack([cos * u0 - sin * u1, sin * u0 + cos * u1], axis=-1).reshape(u.shape)


def rope_back(g, angles):
    gp = g.reshape(g.shape[:-1] + (HD // 2, 2))
    cos = np.cos(angles)[None, :, None, :]
    sin = np.sin(angles)[None, :, None, :]
    g0, g1 = gp[..., 0], gp[..., 1]
    return np.stack([cos * g0 + sin * g1, cos * g1 - sin * g0], axis=-1).reshape(g.shape)


def setup_inputs():
    s = mx_kscale(T)
    uq = mx_kscale(JQ)
    uk = mx_kscale(JK)
    uv = mx_kscale(JK)
    x = bf(np.random.standard_normal((B, T, C)) * s[None, :, None])
    angles = bf(np.random.uniform(-np.pi, np.pi, (T, HD // 2)))
    wq = bf(np.random.standard_normal((C, JQ)) * 0.5 / np.sqrt(C) / uq[None, :])
    wk = bf(np.random.standard_normal((C, JK)) * 0.5 / np.sqrt(C) / uk[None, :])
    wv = bf(np.random.standard_normal((C, JK)) / np.sqrt(C) / uv[None, :])
    st = s.reshape(1, 1, T, 1)
    g0 = bf(np.random.standard_normal((B, NH, T, HD)) * np.exp2(np.random.randint(-6, 1, (B, 1, T, 1))) / st * uq.reshape(1, NH, 1, HD))
    g1 = bf(np.random.standard_normal((B, NKV, T, HD)) * np.exp2(np.random.randint(-6, 1, (B, 1, T, 1))) / st * uk.reshape(1, NKV, 1, HD))
    g2 = bf(np.random.standard_normal((B, NKV, T, HD)) * np.exp2(np.random.randint(-6, 1, (B, 1, T, 1))) / st * uv.reshape(1, NKV, 1, HD))
    return {"x": x, "angles": angles, "wq": wq, "wk": wk, "wv": wv, "grad_0": g0, "grad_1": g1, "grad_2": g2}


def reference(x, angles, wq, wk, wv, grad_0, grad_1, grad_2):
    a = f64(angles)
    dq = rope_back(f64(grad_0).transpose(0, 2, 1, 3), a).reshape(B * T, JQ)
    dk = rope_back(f64(grad_1).transpose(0, 2, 1, 3), a).reshape(B * T, JK)
    dv = f64(grad_2).transpose(0, 2, 1, 3).reshape(B * T, JK)
    dz = np.concatenate([dq, dk, dv], axis=1)
    w = np.concatenate([f64(wq), f64(wk), f64(wv)], axis=1)
    dx = mxq(dz, 1, "e5m2") @ mxq(w, 1, "e4m3").T
    xt = mxq(f64(x).reshape(B * T, C), 0, "e4m3")
    dw = xt.T @ mxq(dz, 0, "e5m2")
    return dx.reshape(B, T, C), dw[:, :JQ], dw[:, JQ:JQ + JK], dw[:, JQ + JK:]

@@ -1,0 +1,397 @@
+import math
+from contextlib import ExitStack
+
+import concourse.mybir as mybir
+from concourse.masks import make_identity
+
+F32 = mybir.dt.float32
+BF16 = mybir.dt.bfloat16
+U32 = mybir.dt.uint32
+U8 = mybir.dt.uint8
+E4 = mybir.dt.float8_e4m3fn_x4
+E5 = mybir.dt.float8_e5m2_x4
+ALU = mybir.AluOpType
+ACT = mybir.ActivationFunctionType
+
+P = 128
+T = 512
+C = 1536
+FEATS = 3072
+FLOPS = 4 * T * C * FEATS
+
+
+def tile_groupqueryatention_pa_v_kernel(
+    tc, x, angles, wq, wk, wv, grad_0, grad_1, grad_2, out_0, out_1, out_2, out_3
+):
+    nc = tc.nc
+    chunks = [(grad_2, 0, wv, 0, out_3), (grad_1, 0, wk, 0, out_2)]
+    for i in range(4):
+        chunks.append((grad_0, 4 * i, wq, 512 * i, out_1))
+    NCH = 6
+
+    with ExitStack() as ctx:
+        const = ctx.enter_context(tc.tile_pool(name="const", bufs=1))
+        keep = ctx.enter_context(tc.tile_pool(name="keep", bufs=1))
+        load = ctx.enter_context(tc.tile_pool(name="load", bufs=6))
+        wload = ctx.enter_context(tc.tile_pool(name="wload", bufs=2))
+        work = ctx.enter_context(tc.tile_pool(name="work", bufs=2))
+        group = ctx.enter_context(tc.tile_pool(name="group", bufs=6))
+        wcode = ctx.enter_context(tc.tile_pool(name="wcode", bufs=2))
+        stage = ctx.enter_context(tc.tile_pool(name="stage", bufs=4))
+        psum = ctx.enter_context(tc.psum_pool(name="psum", bufs=2))
+
+        ident = const.tile([P, P], F32, name="ident")
+        make_identity(nc, ident[:])
+        ctx.enter_context(tc.manual_schedule())
+
+        warm = const.tile([P, 1], F32, name="warm")
+        nc.vector.memset(warm[:], 0.0)
+        warm_out = const.tile([P, 1], F32, name="warm_out")
+        nc.scalar.activation(warm_out[:], warm[:], ACT.Sin)
+
+        ang = const.tile([P, 256], BF16, name="ang")
+        sin_t = const.tile([P, 512], F32, name="sin_t")
+        half_t = const.tile([P, 512], F32, name="half_t")
+        sq_t = const.tile([P, 512], F32, name="sq_t")
+        cos_t = const.tile([P, 512], F32, name="cos_t")
+        xcodes = keep.tile([P, C], U32, name="xcodes", align_bytes=64)
+        xscales = keep.tile([P, C], U8, name="xscales", align_bytes=64)
+        tcodes, tscales, fcodes, fscales = [], [], [], []
+        for i in range(NCH):
+            tcodes.append(keep.tile([P, 512], U32, name="tcodes%d" % i, align_bytes=64))
+            tscales.append(keep.tile([P, 512], U8, name="tscales%d" % i, align_bytes=64))
+            fcodes.append(keep.tile([P, 512], U32, name="fcodes%d" % i, align_bytes=64))
+            fscales.append(keep.tile([P, 512], U8, name="fscales%d" % i, align_bytes=64))
+
+        raw_g, raw_x, raw_w, dz, xg, fg, wg, turn, wc, ws, acc = {}, {}, {}, {}, {}, {}, {}, {}, {}, {}, {}
+        halves = {}
+        stages = {}
+
+        def load_g(i):
+            g, h0 = chunks[i][0], chunks[i][1]
+            t = load.tile([P, 4, 4, P], BF16, name="raw", tag="raw", align_bytes=64)
+            nc.sync.dma_start(
+                out=t[:].rearrange("p h j d -> p h (j d)"),
+                in_=g[0, h0 : h0 + 4].rearrange("h (p j) d -> p h (j d)", j=4),
+            )
+            raw_g[i] = t
+
+        def load_x(k):
+            t = load.tile([P, 4, 512], BF16, name="raw", tag="raw", align_bytes=64)
+            nc.sync.dma_start(
+                out=t[:], in_=x[0, :, 512 * k : 512 * k + 512].rearrange("(p j) c -> p j c", j=4)
+            )
+            raw_x[k] = t
+
+        def load_w(n, part):
+            rows = slice(512 * n, 512 * n + 512)
+            if part < 2:
+                src = chunks[part][2][rows, :]
+                width = 512
+            else:
+                src = wq[rows, 1024 * (part - 2) : 1024 * (part - 1)]
+                width = 1024
+            t = wload.tile([P, 4, width], BF16, name="w%d" % part, tag="w%d" % part, align_bytes=64)
+            nc.sync.dma_start(out=t[:], in_=src.rearrange("(p r) f -> p r f", r=4))
+            raw_w[(n, part)] = t
+
+        def w_words(n, i):
+            if i < 2:
+                return raw_w[(n, i)][:].bitcast(F32), 0
+            return raw_w[(n, 2 + (i - 2) // 2)][:].bitcast(F32), 256 * ((i - 2) % 2)
+
+        def copy(on_vector, out, in_):
+            if on_vector:
+                nc.vector.tensor_copy(out=out, in_=in_)
+            else:
+                nc.scalar.copy(out=out, in_=in_)
+
+        def quantize(codes, scales, src, fmt):
+            nc.vector.quantize_mx(out=codes.bitcast(fmt), scales=scales, in_=src)
+
+        def x_group(k, on_vector):
+            t = group.tile([P, 2048], BF16, name="grp", tag="grp", align_bytes=64)
+            copy(
+                on_vector,
+                t[:].rearrange("p (r q j) -> p r q j", r=4, j=4),
+                raw_x[k][:].rearrange("p j (q r) -> p r q j", r=4),
+            )
+            xg[k] = t
+
+        def x_quant(k):
+            cols = slice(512 * k, 512 * k + 512)
+            quantize(xcodes[:, cols], xscales[:, cols], xg[k][:], E4)
+
+        def dz_tile(i):
+            dz[i] = work.tile([P, 4, P, 4], BF16, name="dz", tag="dz", align_bytes=64)
+
+        def dv_group():
+            dz_tile(0)
+            nc.vector.tensor_copy(
+                out=dz[0][:].rearrange("p t (h q) j -> p t h q j", h=4),
+                in_=raw_g[0][:].rearrange("p h j (q t) -> p t h q j", t=4),
+            )
+
+        def rope_mul(i, hh, which):
+            t = work.tile([P, 4, 2, P], F32, name="prod%d" % which, tag="prod%d" % which)
+            table = (cos_t, sin_t)[which]
+            nc.vector.tensor_tensor(
+                out=t[:].rearrange("p j h d -> p h j d"),
+                in0=raw_g[i][:, 2 * hh : 2 * hh + 2],
+                in1=table[:].rearrange("p (j d) -> p j d", j=4).unsqueeze(1).to_broadcast([P, 2, 4, P]),
+                op=ALU.mult,
+            )
+            halves[(i, hh, which)] = t
+
+        def rope_add(i, hh, e):
+            v0 = halves[(i, hh, 0)][:].rearrange("p j h (q t) -> p t (h q) j", t=4)
+            v1 = halves[(i, hh, 1)][:].rearrange("p j h (q t) -> p t (h q) j", t=4)
+            nc.vector.tensor_tensor(
+                out=dz[i][:, e::2, 64 * hh : 64 * hh + 64, :],
+                in0=v0[:, e::2],
+                in1=v1[:, 1 - e :: 2],
+                op=(ALU.add, ALU.subtract)[e],
+            )
+
+        def t_quant(i):
+            quantize(tcodes[i][:], tscales[i][:], dz[i][:].rearrange("p t m j -> p (t m j)"), E5)
+
+        def d_turn(i, a):
+            bank = psum.tile([P, 512], F32, name="turn", tag="turn")
+            words = dz[i][:].rearrange("p t m j -> p (t m j)").bitcast(F32)
+            for t in range(4):
+                nc.tensor.transpose(
+                    bank[:, 128 * t : 128 * t + 128], words[:, 256 * t + a : 256 * t + 256 : 2], ident[:]
+                )
+            turn[("d", i, a)] = bank
+
+        def d_copy(i, a, on_vector):
+            if a == 0:
+                fg[i] = group.tile([P, 2048], BF16, name="grp", tag="grp", align_bytes=64)
+            copy(
+                on_vector,
+                fg[i][:, 1024 * a : 1024 * a + 1024].rearrange("p (e q t) -> p e q t", e=2, t=4),
+                turn[("d", i, a)][:].bitcast(BF16).rearrange("p (t q e) -> p e q t", t=4, e=2),
+            )
+
+        def f_quant(i):
+            quantize(fcodes[i][:], fscales[i][:], fg[i][:], E5)
+
+        def w_turn(n, i, b):
+            bank = psum.tile([P, 512], F32, name="turn", tag="turn")
+            words, w0 = w_words(n, i)
+            for u in range(2):
+                for k in range(2):
+                    at = 256 * u + 128 * k
+                    nc.tensor.transpose(
+                        bank[:, at : at + 128], words[:, 2 * b + k, w0 + u : w0 + 256 : 2], ident[:]
+                    )
+            turn[("w", n, i, b)] = bank
+
+        def w_copy(n, i, b, on_vector):
+            if b == 0:
+                wg[(n, i)] = group.tile([P, 2048], BF16, name="grp", tag="grp", align_bytes=64)
+            copy(
+                on_vector,
+                wg[(n, i)][:].bitcast(F32)[:, 512 * b : 512 * b + 512].rearrange("p (c u) -> p c u", u=2),
+                turn[("w", n, i, b)][:].rearrange("p (u c) -> p c u", u=2),
+            )
+
+        def w_quant(n, i):
+            wc[(n, i)] = wcode.tile([P, 512], U32, name="wc%d" % i, tag="wc%d" % i, align_bytes=64)
+            ws[(n, i)] = wcode.tile([P, 512], U8, name="ws%d" % i, tag="ws%d" % i, align_bytes=64)
+            quantize(wc[(n, i)][:], ws[(n, i)][:], wg[(n, i)][:], E4)
+
+        def acc_pass(n, i):
+            for j in range(4):
+                if i == 0:
+                    acc[(n, j)] = psum.tile([P, 512], F32, name="acc", tag="acc", bufs=4)
+                nc.tensor.matmul_mx(
+                    out=acc[(n, j)][:],
+                    lhsT=fcodes[i][:, 128 * j : 128 * j + 128].bitcast(E5),
+                    lhsT_scale=fscales[i][:, 128 * j : 128 * j + 128],
+                    rhs=wc[(n, i)][:].bitcast(E4),
+                    rhs_scale=ws[(n, i)][:],
+                    start=(i == 0),
+                    stop=(i == NCH - 1),
+                )
+
+        def acc_out(n, j, on_vector):
+            if j == 0:
+                stages[n] = stage.tile([P, 4, 512], F32, name="stage", tag="stage")
+            copy(
+                on_vector,
+                stages[n][:, j, :].rearrange("p (q r) -> p q r", r=4),
+                acc[(n, j)][:].rearrange("p (r q) -> p q r", r=4),
+            )
+            if j == 3:
+                nc.gpsimd.dma_start(
+                    out=out_0[0, :, 512 * n : 512 * n + 512].rearrange("(p j) c -> p j c", j=4),
+                    in_=stages[n][:],
+                )
+
+        dw_bank = {}
+
+        def dw_mm(i, m):
+            bank = psum.tile([P, 512], F32, name="dwout", tag="dwout")
+            nc.tensor.matmul_mx(
+                out=bank[:],
+                lhsT=xcodes[:, 128 * m : 128 * m + 128].bitcast(E4),
+                lhsT_scale=xscales[:, 128 * m : 128 * m + 128],
+                rhs=tcodes[i][:].bitcast(E5),
+                rhs_scale=tscales[i][:],
+                start=True,
+                stop=True,
+            )
+            dw_bank[(i, m)] = bank
+
+        def dw_out(i, m, on_vector):
+            r, k = m % 4, m // 4
+            if r == 0:
+                stages["dw"] = stage.tile([P, 4, 512], F32, name="stage", tag="stage")
+            st = stages["dw"]
+            copy(
+                on_vector,
+                st[:, r, :].rearrange("p (m t) -> p m t", t=4),
+                dw_bank[(i, m)][:].rearrange("p (t m) -> p m t", t=4),
+            )
+            if r == 3:
+                col, out = chunks[i][3], chunks[i][4]
+                nc.gpsimd.dma_start(
+                    out=out[512 * k : 512 * k + 512, col : col + 512].rearrange("(q r) f -> q r f", r=4),
+                    in_=st[:],
+                )
+
+        nc.sync.dma_start(out=ang[:], in_=angles.rearrange("(p j) i -> p (j i)", j=4))
+        load_g(0)
+        load_x(0)
+        load_x(1)
+        load_x(2)
+        load_g(1)
+        load_g(2)
+        load_w(0, 0)
+        load_w(0, 1)
+        late_loads = {
+            1: [lambda: load_g(3), lambda: load_w(0, 2)],
+            2: [lambda: load_g(4), lambda: load_w(0, 3)],
+            3: [lambda: load_g(5), lambda: load_w(1, 0), lambda: load_w(1, 1)],
+            4: [lambda: load_w(1, 2)],
+            5: [lambda: load_w(1, 3), lambda: load_w(2, 0), lambda: load_w(2, 1)],
+        }
+
+        twice = ang[:].unsqueeze(2).to_broadcast([P, 256, 2])
+        nc.scalar.activation(sin_t[:].rearrange("p (a b) -> p a b", b=2), twice, ACT.Sin)
+        nc.scalar.activation(half_t[:].rearrange("p (a b) -> p a b", b=2), twice, ACT.Sin, scale=0.5)
+        dv_group()
+        x_group(0, True)
+        x_group(1, False)
+        t_quant(0)
+        x_quant(0)
+        nc.vector.tensor_tensor(out=sq_t[:], in0=half_t[:], in1=half_t[:], op=ALU.mult)
+        x_group(2, True)
+        nc.vector.tensor_scalar(out=cos_t[:], in0=sq_t[:], scalar1=-2.0, scalar2=1.0, op0=ALU.mult, op1=ALU.add)
+        x_quant(1)
+
+        dw_list = [(i, m) for i in range(NCH) for m in range(12)]
+        dw_at = [0]
+
+        def dw(count, on_vector=(False, False)):
+            pair = dw_list[dw_at[0] : dw_at[0] + count]
+            dw_at[0] += count
+            for i, m in pair:
+                dw_mm(i, m)
+            return [lambda i=i, m=m, v=v: dw_out(i, m, v) for (i, m), v in zip(pair, on_vector)]
+
+        def run(items):
+            for f in items:
+                f()
+
+        w_in_slot = {2: [0, 1], 3: [2], 4: [3], 5: [4]}
+        acc_in_slot = {3: [0, 1], 4: [2], 5: [3]}
+        dw_in_slot = {1: 12, 2: 8, 3: 8, 4: 8, 5: 8}
+        extra = {
+            1: [lambda: x_quant(2), None],
+            2: [None, lambda: w_quant(0, 0)],
+            3: [lambda: w_quant(0, 1), None],
+            4: [lambda: w_quant(0, 2), None],
+            5: [lambda: w_quant(0, 3), None],
+        }
+        for i in range(1, NCH):
+            run(late_loads[i])
+            dz_tile(i)
+            left = dw_in_slot[i]
+            rope_mul(i, 0, 0)
+            if i > 1:
+                t_quant(i - 1)
+            rope_mul(i, 0, 1)
+            d_turn(i - 1, 0)
+            d_turn(i - 1, 1)
+            d_copy(i - 1, 0, False)
+            outs = dw(2)
+            d_copy(i - 1, 1, False)
+            run(outs)
+            left -= 2
+            if extra[i][0]:
+                extra[i][0]()
+            rope_mul(i, 1, 0)
+            for w in w_in_slot.get(i, []):
+                w_turn(0, w, 0)
+                w_turn(0, w, 1)
+                outs = dw(2)
+                w_copy(0, w, 0, False)
+                run(outs)
+                w_copy(0, w, 1, False)
+                left -= 2
+            rope_add(i, 0, 0)
+            rope_mul(i, 1, 1)
+            run(dw(2))
+            left -= 2
+            rope_add(i, 0, 1)
+            f_quant(i - 1)
+            rope_add(i, 1, 0)
+            if extra[i][1]:
+                extra[i][1]()
+            rope_add(i, 1, 1)
+            for a in acc_in_slot.get(i, []):
+                acc_pass(0, a)
+            while left > 0:
+                run(dw(2))
+                left -= 2
+
+        units = [(0, 5)] + [(1, i) for i in range(NCH)] + [(2, i) for i in range(NCH)]
+        t_quant(5)
+        d_turn(5, 0)
+        d_turn(5, 1)
+        outs = dw(2, (True, False))
+        d_copy(5, 0, False)
+        d_copy(5, 1, True)
+        run(outs)
+        w_quant(0, 4)
+        b_loads = [lambda: load_w(2, 2), lambda: load_w(2, 3)]
+        for k in range(len(units) + 2):
+            if k == 1:
+                run(b_loads)
+            if k < len(units):
+                n, i = units[k]
+                w_turn(n, i, 0)
+                w_turn(n, i, 1)
+            if k >= 2:
+                acc_pass(*units[k - 2])
+            elif k == 0:
+                acc_pass(0, 4)
+            left = len(dw_list) - dw_at[0]
+            outs = dw(2, (False, k % 3 == 2)) if left else []
+            if k < len(units):
+                w_copy(n, i, 0, False)
+            if k == 0:
+                f_quant(5)
+            if 1 <= k <= len(units):
+                w_quant(*units[k - 1])
+            if k < len(units):
+                w_copy(n, i, 1, True)
+            run(outs)
+            if k >= 2 and units[k - 2][1] == NCH - 1:
+                for j in range(4):
+                    acc_out(units[k - 2][0], j, j % 2 == 1)
+        while dw_at[0] < len(dw_list):
+            run(dw(2, (False, True)))

@@ -37,7 +37,8 @@ def tile_groupqueryatention_pa_v_kernel(
         work = ctx.enter_context(tc.tile_pool(name="work", bufs=2))
         group = ctx.enter_context(tc.tile_pool(name="group", bufs=6))
         wcode = ctx.enter_context(tc.tile_pool(name="wcode", bufs=2))
-        stage = ctx.enter_context(tc.tile_pool(name="stage", bufs=4))
+        stage = ctx.enter_context(tc.tile_pool(name="stage", bufs=3))
+        ostage = ctx.enter_context(tc.tile_pool(name="ostage", bufs=6))
         psum = ctx.enter_context(tc.psum_pool(name="psum", bufs=2))
 
         ident = const.tile([P, P], F32, name="ident")
@@ -50,10 +51,10 @@ def tile_groupqueryatention_pa_v_kernel(
         nc.scalar.activation(warm_out[:], warm[:], ACT.Sin)
 
         ang = const.tile([P, 256], BF16, name="ang")
-        sin_t = const.tile([P, 512], F32, name="sin_t")
-        half_t = const.tile([P, 512], F32, name="half_t")
-        sq_t = const.tile([P, 512], F32, name="sq_t")
-        cos_t = const.tile([P, 512], F32, name="cos_t")
+        sin_t = const.tile([P, 2, P], F32, name="sin_t")
+        half_t = const.tile([P, 2, P], F32, name="half_t")
+        sq_t = const.tile([P, 2, P], F32, name="sq_t")
+        cos_t = const.tile([P, 2, P], F32, name="cos_t")
         xcodes = keep.tile([P, C], U32, name="xcodes", align_bytes=64)
         xscales = keep.tile([P, C], U8, name="xscales", align_bytes=64)
         tcodes, tscales, fcodes, fscales = [], [], [], []
@@ -132,24 +133,23 @@ def tile_groupqueryatention_pa_v_kernel(
                 in_=raw_g[0][:].rearrange("p h j (q t) -> p t h q j", t=4),
             )
 
-        def rope_mul(i, hh, which):
-            t = work.tile([P, 4, 2, P], F32, name="prod%d" % which, tag="prod%d" % which)
+        def rope_mul(i, s, which):
+            t = work.tile([P, 2, 4, P], F32, name="prod%d" % which, tag="prod%d" % which)
             table = (cos_t, sin_t)[which]
             nc.vector.tensor_tensor(
-                out=t[:].rearrange("p j h d -> p h j d"),
-                in0=raw_g[i][:, 2 * hh : 2 * hh + 2],
-                in1=table[:].rearrange("p (j d) -> p j d", j=4).unsqueeze(1).to_broadcast([P, 2, 4, P]),
+                out=t[:],
+                in0=raw_g[i][:].rearrange("p h j (q t) -> p t h (j q)", t=4)[:, 2 * s : 2 * s + 2],
+                in1=table[:, s : s + 1, :].unsqueeze(2).to_broadcast([P, 2, 4, P]),
                 op=ALU.mult,
             )
-            halves[(i, hh, which)] = t
+            halves[(i, s, which)] = t
 
-        def rope_add(i, hh, e):
-            v0 = halves[(i, hh, 0)][:].rearrange("p j h (q t) -> p t (h q) j", t=4)
-            v1 = halves[(i, hh, 1)][:].rearrange("p j h (q t) -> p t (h q) j", t=4)
+        def rope_add(i, t):
+            s, e = t // 2, t % 2
             nc.vector.tensor_tensor(
-                out=dz[i][:, e::2, 64 * hh : 64 * hh + 64, :],
-                in0=v0[:, e::2],
-                in1=v1[:, 1 - e :: 2],
+                out=dz[i][:, t].rearrange("p (h q) j -> p h q j", h=4),
+                in0=halves[(i, s, 0)][:, e].rearrange("p h (j q) -> p h q j", j=4),
+                in1=halves[(i, s, 1)][:, 1 - e].rearrange("p h (j q) -> p h q j", j=4),
                 op=(ALU.add, ALU.subtract)[e],
             )
 
@@ -202,8 +202,8 @@ def tile_groupqueryatention_pa_v_kernel(
             ws[(n, i)] = wcode.tile([P, 512], U8, name="ws%d" % i, tag="ws%d" % i, align_bytes=64)
             quantize(wc[(n, i)][:], ws[(n, i)][:], wg[(n, i)][:], E4)
 
-        def acc_pass(n, i):
-            for j in range(4):
+        def acc_pass(n, i, js=(0, 1, 2, 3)):
+            for j in js:
                 if i == 0:
                     acc[(n, j)] = psum.tile([P, 512], F32, name="acc", tag="acc", bufs=4)
                 nc.tensor.matmul_mx(
@@ -217,18 +217,16 @@ def tile_groupqueryatention_pa_v_kernel(
                 )
 
         def acc_out(n, j, on_vector):
-            if j == 0:
-                stages[n] = stage.tile([P, 4, 512], F32, name="stage", tag="stage")
+            st = ostage.tile([P, 512], F32, name="ostage", tag="ostage")
             copy(
                 on_vector,
-                stages[n][:, j, :].rearrange("p (q r) -> p q r", r=4),
+                st[:].rearrange("p (q r) -> p q r", r=4),
                 acc[(n, j)][:].rearrange("p (r q) -> p q r", r=4),
             )
-            if j == 3:
-                nc.gpsimd.dma_start(
-                    out=out_0[0, :, 512 * n : 512 * n + 512].rearrange("(p j) c -> p j c", j=4),
-                    in_=stages[n][:],
-                )
+            nc.gpsimd.dma_start(
+                out=out_0[0, :, 512 * n : 512 * n + 512].rearrange("(p j) c -> p j c", j=4)[:, j, :],
+                in_=st[:],
+            )
 
         dw_bank = {}
 
@@ -268,29 +266,28 @@ def tile_groupqueryatention_pa_v_kernel(
         load_x(1)
         load_x(2)
         load_g(1)
-        load_g(2)
         load_w(0, 0)
         load_w(0, 1)
+        load_g(2)
+        load_w(0, 2)
         late_loads = {
-            1: [lambda: load_g(3), lambda: load_w(0, 2)],
-            2: [lambda: load_g(4), lambda: load_w(0, 3)],
-            3: [lambda: load_g(5), lambda: load_w(1, 0), lambda: load_w(1, 1)],
-            4: [lambda: load_w(1, 2)],
-            5: [lambda: load_w(1, 3), lambda: load_w(2, 0), lambda: load_w(2, 1)],
+            1: [lambda: load_w(0, 3), lambda: load_g(3)],
+            2: [lambda: load_w(1, 0), lambda: load_w(1, 1), lambda: load_g(4), lambda: load_w(1, 2)],
+            3: [lambda: load_g(5), lambda: load_w(1, 3), lambda: load_w(2, 0)],
+            4: [lambda: load_w(2, 1), lambda: load_w(2, 2)],
+            5: [lambda: load_w(2, 3)],
         }
 
-        twice = ang[:].unsqueeze(2).to_broadcast([P, 256, 2])
-        nc.scalar.activation(sin_t[:].rearrange("p (a b) -> p a b", b=2), twice, ACT.Sin)
-        nc.scalar.activation(half_t[:].rearrange("p (a b) -> p a b", b=2), twice, ACT.Sin, scale=0.5)
+        by_s = ang[:].rearrange("p (a s) -> p s a", s=2)
+        nc.scalar.activation(sin_t[:], by_s, ACT.Sin)
+        nc.scalar.activation(half_t[:], by_s, ACT.Sin, scale=0.5)
         dv_group()
         x_group(0, True)
         x_group(1, False)
         t_quant(0)
         x_quant(0)
         nc.vector.tensor_tensor(out=sq_t[:], in0=half_t[:], in1=half_t[:], op=ALU.mult)
-        x_group(2, True)
         nc.vector.tensor_scalar(out=cos_t[:], in0=sq_t[:], scalar1=-2.0, scalar2=1.0, op0=ALU.mult, op1=ALU.add)
-        x_quant(1)
 
         dw_list = [(i, m) for i in range(NCH) for m in range(12)]
         dw_at = [0]
@@ -306,24 +303,34 @@ def tile_groupqueryatention_pa_v_kernel(
             for f in items:
                 f()
 
-        w_in_slot = {2: [0, 1], 3: [2], 4: [3], 5: [4]}
-        acc_in_slot = {3: [0, 1], 4: [2], 5: [3]}
-        dw_in_slot = {1: 12, 2: 8, 3: 8, 4: 8, 5: 8}
-        extra = {
-            1: [lambda: x_quant(2), None],
-            2: [None, lambda: w_quant(0, 0)],
-            3: [lambda: w_quant(0, 1), None],
-            4: [lambda: w_quant(0, 2), None],
-            5: [lambda: w_quant(0, 3), None],
+        w_in_slot = {
+            1: [(0, 0), (0, 1)],
+            2: [(0, 2), (0, 3), (0, 4)],
+            3: [(0, 5), (1, 0), (1, 1)],
+            4: [(1, 2), (1, 3), (1, 4)],
+            5: [(1, 5), (2, 0), (2, 1)],
         }
+        dw_in_slot = {1: 10, 2: 8, 3: 6, 4: 6, 5: 6}
+        pending = []
+
+        def w_quant_next():
+            if pending:
+                w_quant(*pending.pop(0))
+
         for i in range(1, NCH):
             run(late_loads[i])
             dz_tile(i)
             left = dw_in_slot[i]
+            units = list(w_in_slot[i])
             rope_mul(i, 0, 0)
             if i > 1:
                 t_quant(i - 1)
+            else:
+                x_quant(1)
             rope_mul(i, 0, 1)
+            if i == 1:
+                x_group(2, True)
+            w_quant_next()
             d_turn(i - 1, 0)
             d_turn(i - 1, 1)
             d_copy(i - 1, 0, False)
@@ -331,67 +338,72 @@ def tile_groupqueryatention_pa_v_kernel(
             d_copy(i - 1, 1, False)
             run(outs)
             left -= 2
-            if extra[i][0]:
-                extra[i][0]()
             rope_mul(i, 1, 0)
-            for w in w_in_slot.get(i, []):
-                w_turn(0, w, 0)
-                w_turn(0, w, 1)
-                outs = dw(2)
-                w_copy(0, w, 0, False)
-                run(outs)
-                w_copy(0, w, 1, False)
-                left -= 2
-            rope_add(i, 0, 0)
-            rope_mul(i, 1, 1)
-            run(dw(2))
-            left -= 2
-            rope_add(i, 0, 1)
-            f_quant(i - 1)
-            rope_add(i, 1, 0)
-            if extra[i][1]:
-                extra[i][1]()
-            rope_add(i, 1, 1)
-            for a in acc_in_slot.get(i, []):
-                acc_pass(0, a)
+            if i == 1:
+                x_quant(2)
+            rope_add(i, 0)
+            for step in range(3):
+                if units:
+                    n, w = units.pop(0)
+                    w_turn(n, w, 0)
+                    w_turn(n, w, 1)
+                    if step == 0 and i >= 2:
+                        acc_pass(0, i - 2)
+                    count = min(2, left)
+                    outs = dw(count)
+                    left -= count
+                    w_copy(n, w, 0, False)
+                    w_copy(n, w, 1, False)
+                    run(outs)
+                    pending.append((n, w))
+                if step == 0:
+                    rope_mul(i, 1, 1)
+                    rope_add(i, 1)
+                    f_quant(i - 1)
+                if step == 1:
+                    rope_add(i, 2)
+                    w_quant_next()
+                    rope_add(i, 3)
+                    w_quant_next()
             while left > 0:
                 run(dw(2))
                 left -= 2
 
-        units = [(0, 5)] + [(1, i) for i in range(NCH)] + [(2, i) for i in range(NCH)]
         t_quant(5)
         d_turn(5, 0)
         d_turn(5, 1)
-        outs = dw(2, (True, False))
+        outs = dw(2)
+        w_quant_next()
         d_copy(5, 0, False)
         d_copy(5, 1, True)
         run(outs)
-        w_quant(0, 4)
-        b_loads = [lambda: load_w(2, 2), lambda: load_w(2, 3)]
-        for k in range(len(units) + 2):
-            if k == 1:
-                run(b_loads)
-            if k < len(units):
-                n, i = units[k]
-                w_turn(n, i, 0)
-                w_turn(n, i, 1)
-            if k >= 2:
-                acc_pass(*units[k - 2])
-            elif k == 0:
-                acc_pass(0, 4)
-            left = len(dw_list) - dw_at[0]
-            outs = dw(2, (False, k % 3 == 2)) if left else []
-            if k < len(units):
-                w_copy(n, i, 0, False)
+        tail_units = [(2, 2), (2, 3), (2, 4), (2, 5)]
+        for k, (n, w) in enumerate(tail_units):
+            w_turn(n, w, 0)
+            w_turn(n, w, 1)
             if k == 0:
+                acc_pass(0, 4)
+            if k == 1:
                 f_quant(5)
-            if 1 <= k <= len(units):
-                w_quant(*units[k - 1])
-            if k < len(units):
-                w_copy(n, i, 1, True)
+            outs = dw(2, (False, True))
+            w_copy(n, w, 0, False)
+            w_copy(n, w, 1, True)
             run(outs)
-            if k >= 2 and units[k - 2][1] == NCH - 1:
+            pending.append((n, w))
+            if k == 1:
+                acc_pass(0, 5)
+            if k == 2:
                 for j in range(4):
-                    acc_out(units[k - 2][0], j, j % 2 == 1)
+                    acc_out(0, j, j % 2 == 1)
+            w_quant_next()
+        while pending:
+            w_quant_next()
+        for k in range(8):
+            n, j = 1 + k // 4, k % 4
+            for i in range(NCH):
+                acc_pass(n, i, (j,))
+                if i % 2 == 1:
+                    run(dw(min(1, len(dw_list) - dw_at[0]), (dw_at[0] % 2 == 1,)))
+            acc_out(n, j, k % 2 == 1)
         while dw_at[0] < len(dw_list):
             run(dw(2, (False, True)))

import math
from contextlib import ExitStack

import concourse.mybir as mybir
from concourse.masks import make_identity

F32 = mybir.dt.float32
BF16 = mybir.dt.bfloat16
U32 = mybir.dt.uint32
U8 = mybir.dt.uint8
E4 = mybir.dt.float8_e4m3fn_x4
E5 = mybir.dt.float8_e5m2_x4
ALU = mybir.AluOpType
ACT = mybir.ActivationFunctionType

P = 128
T = 512
C = 1536
FEATS = 3072
FLOPS = 4 * T * C * FEATS


def tile_groupqueryatention_pa_v_kernel(
    tc, x, angles, wq, wk, wv, grad_0, grad_1, grad_2, out_0, out_1, out_2, out_3
):
    nc = tc.nc
    chunks = [(grad_2, 0, wv, 0, out_3), (grad_1, 0, wk, 0, out_2)]
    for i in range(4):
        chunks.append((grad_0, 4 * i, wq, 512 * i, out_1))
    NCH = 6

    with ExitStack() as ctx:
        const = ctx.enter_context(tc.tile_pool(name="const", bufs=1))
        keep = ctx.enter_context(tc.tile_pool(name="keep", bufs=1))
        load = ctx.enter_context(tc.tile_pool(name="load", bufs=6))
        wload = ctx.enter_context(tc.tile_pool(name="wload", bufs=2))
        work = ctx.enter_context(tc.tile_pool(name="work", bufs=2))
        group = ctx.enter_context(tc.tile_pool(name="group", bufs=6))
        wcode = ctx.enter_context(tc.tile_pool(name="wcode", bufs=2))
        stage = ctx.enter_context(tc.tile_pool(name="stage", bufs=3))
        ostage = ctx.enter_context(tc.tile_pool(name="ostage", bufs=6))
        psum = ctx.enter_context(tc.psum_pool(name="psum", bufs=2))

        ident = const.tile([P, P], F32, name="ident")
        make_identity(nc, ident[:])
        ctx.enter_context(tc.manual_schedule())

        warm = const.tile([P, 1], F32, name="warm")
        nc.vector.memset(warm[:], 0.0)
        warm_out = const.tile([P, 1], F32, name="warm_out")
        nc.scalar.activation(warm_out[:], warm[:], ACT.Sin)

        ang = const.tile([P, 256], BF16, name="ang")
        sin_t = const.tile([P, 2, P], F32, name="sin_t")
        half_t = const.tile([P, 2, P], F32, name="half_t")
        sq_t = const.tile([P, 2, P], F32, name="sq_t")
        cos_t = const.tile([P, 2, P], F32, name="cos_t")
        xcodes = keep.tile([P, C], U32, name="xcodes", align_bytes=64)
        xscales = keep.tile([P, C], U8, name="xscales", align_bytes=64)
        tcodes, tscales, fcodes, fscales = [], [], [], []
        for i in range(NCH):
            tcodes.append(keep.tile([P, 512], U32, name="tcodes%d" % i, align_bytes=64))
            tscales.append(keep.tile([P, 512], U8, name="tscales%d" % i, align_bytes=64))
            fcodes.append(keep.tile([P, 512], U32, name="fcodes%d" % i, align_bytes=64))
            fscales.append(keep.tile([P, 512], U8, name="fscales%d" % i, align_bytes=64))

        raw_g, raw_x, raw_w, dz, xg, fg, wg, turn, wc, ws, acc = {}, {}, {}, {}, {}, {}, {}, {}, {}, {}, {}
        halves = {}
        stages = {}

        def load_g(i):
            g, h0 = chunks[i][0], chunks[i][1]
            t = load.tile([P, 4, 4, P], BF16, name="raw", tag="raw", align_bytes=64)
            nc.sync.dma_start(
                out=t[:].rearrange("p h j d -> p h (j d)"),
                in_=g[0, h0 : h0 + 4].rearrange("h (p j) d -> p h (j d)", j=4),
            )
            raw_g[i] = t

        def load_x(k):
            t = load.tile([P, 4, 512], BF16, name="raw", tag="raw", align_bytes=64)
            nc.sync.dma_start(
                out=t[:], in_=x[0, :, 512 * k : 512 * k + 512].rearrange("(p j) c -> p j c", j=4)
            )
            raw_x[k] = t

        def load_w(n, part):
            rows = slice(512 * n, 512 * n + 512)
            if part < 2:
                src = chunks[part][2][rows, :]
                width = 512
            else:
                src = wq[rows, 1024 * (part - 2) : 1024 * (part - 1)]
                width = 1024
            t = wload.tile([P, 4, width], BF16, name="w%d" % part, tag="w%d" % part, align_bytes=64)
            nc.sync.dma_start(out=t[:], in_=src.rearrange("(p r) f -> p r f", r=4))
            raw_w[(n, part)] = t

        def w_words(n, i):
            if i < 2:
                return raw_w[(n, i)][:].bitcast(F32), 0
            return raw_w[(n, 2 + (i - 2) // 2)][:].bitcast(F32), 256 * ((i - 2) % 2)

        def copy(on_vector, out, in_):
            if on_vector:
                nc.vector.tensor_copy(out=out, in_=in_)
            else:
                nc.scalar.copy(out=out, in_=in_)

        def quantize(codes, scales, src, fmt):
            nc.vector.quantize_mx(out=codes.bitcast(fmt), scales=scales, in_=src)

        def x_group(k, on_vector):
            t = group.tile([P, 2048], BF16, name="grp", tag="grp", align_bytes=64)
            copy(
                on_vector,
                t[:].rearrange("p (r q j) -> p r q j", r=4, j=4),
                raw_x[k][:].rearrange("p j (q r) -> p r q j", r=4),
            )
            xg[k] = t

        def x_quant(k):
            cols = slice(512 * k, 512 * k + 512)
            quantize(xcodes[:, cols], xscales[:, cols], xg[k][:], E4)

        def dz_tile(i):
            dz[i] = work.tile([P, 4, P, 4], BF16, name="dz", tag="dz", align_bytes=64)

        def dv_group():
            dz_tile(0)
            nc.vector.tensor_copy(
                out=dz[0][:].rearrange("p t (h q) j -> p t h q j", h=4),
                in_=raw_g[0][:].rearrange("p h j (q t) -> p t h q j", t=4),
            )

        def rope_mul(i, s, which):
            t = work.tile([P, 2, 4, P], F32, name="prod%d" % which, tag="prod%d" % which)
            table = (cos_t, sin_t)[which]
            nc.vector.tensor_tensor(
                out=t[:],
                in0=raw_g[i][:].rearrange("p h j (q t) -> p t h (j q)", t=4)[:, 2 * s : 2 * s + 2],
                in1=table[:, s : s + 1, :].unsqueeze(2).to_broadcast([P, 2, 4, P]),
                op=ALU.mult,
            )
            halves[(i, s, which)] = t

        def rope_add(i, t):
            s, e = t // 2, t % 2
            nc.vector.tensor_tensor(
                out=dz[i][:, t].rearrange("p (h q) j -> p h q j", h=4),
                in0=halves[(i, s, 0)][:, e].rearrange("p h (j q) -> p h q j", j=4),
                in1=halves[(i, s, 1)][:, 1 - e].rearrange("p h (j q) -> p h q j", j=4),
                op=(ALU.add, ALU.subtract)[e],
            )

        def t_quant(i):
            quantize(tcodes[i][:], tscales[i][:], dz[i][:].rearrange("p t m j -> p (t m j)"), E5)

        def d_turn(i, a):
            bank = psum.tile([P, 512], F32, name="turn", tag="turn")
            words = dz[i][:].rearrange("p t m j -> p (t m j)").bitcast(F32)
            for t in range(4):
                nc.tensor.transpose(
                    bank[:, 128 * t : 128 * t + 128], words[:, 256 * t + a : 256 * t + 256 : 2], ident[:]
                )
            turn[("d", i, a)] = bank

        def d_copy(i, a, on_vector):
            if a == 0:
                fg[i] = group.tile([P, 2048], BF16, name="grp", tag="grp", align_bytes=64)
            copy(
                on_vector,
                fg[i][:, 1024 * a : 1024 * a + 1024].rearrange("p (e q t) -> p e q t", e=2, t=4),
                turn[("d", i, a)][:].bitcast(BF16).rearrange("p (t q e) -> p e q t", t=4, e=2),
            )

        def f_quant(i):
            quantize(fcodes[i][:], fscales[i][:], fg[i][:], E5)

        def w_turn(n, i, b):
            bank = psum.tile([P, 512], F32, name="turn", tag="turn")
            words, w0 = w_words(n, i)
            for u in range(2):
                for k in range(2):
                    at = 256 * u + 128 * k
                    nc.tensor.transpose(
                        bank[:, at : at + 128], words[:, 2 * b + k, w0 + u : w0 + 256 : 2], ident[:]
                    )
            turn[("w", n, i, b)] = bank

        def w_copy(n, i, b, on_vector):
            if b == 0:
                wg[(n, i)] = group.tile([P, 2048], BF16, name="grp", tag="grp", align_bytes=64)
            copy(
                on_vector,
                wg[(n, i)][:].bitcast(F32)[:, 512 * b : 512 * b + 512].rearrange("p (c u) -> p c u", u=2),
                turn[("w", n, i, b)][:].rearrange("p (u c) -> p c u", u=2),
            )

        def w_quant(n, i):
            wc[(n, i)] = wcode.tile([P, 512], U32, name="wc%d" % i, tag="wc%d" % i, align_bytes=64)
            ws[(n, i)] = wcode.tile([P, 512], U8, name="ws%d" % i, tag="ws%d" % i, align_bytes=64)
            quantize(wc[(n, i)][:], ws[(n, i)][:], wg[(n, i)][:], E4)

        def acc_pass(n, i, js=(0, 1, 2, 3)):
            for j in js:
                if i == 0:
                    acc[(n, j)] = psum.tile([P, 512], F32, name="acc", tag="acc", bufs=4)
                nc.tensor.matmul_mx(
                    out=acc[(n, j)][:],
                    lhsT=fcodes[i][:, 128 * j : 128 * j + 128].bitcast(E5),
                    lhsT_scale=fscales[i][:, 128 * j : 128 * j + 128],
                    rhs=wc[(n, i)][:].bitcast(E4),
                    rhs_scale=ws[(n, i)][:],
                    start=(i == 0),
                    stop=(i == NCH - 1),
                )

        def acc_out(n, j, on_vector):
            st = ostage.tile([P, 512], F32, name="ostage", tag="ostage")
            copy(
                on_vector,
                st[:].rearrange("p (q r) -> p q r", r=4),
                acc[(n, j)][:].rearrange("p (r q) -> p q r", r=4),
            )
            nc.gpsimd.dma_start(
                out=out_0[0, :, 512 * n : 512 * n + 512].rearrange("(p j) c -> p j c", j=4)[:, j, :],
                in_=st[:],
            )

        dw_bank = {}

        def dw_mm(i, m):
            bank = psum.tile([P, 512], F32, name="dwout", tag="dwout")
            nc.tensor.matmul_mx(
                out=bank[:],
                lhsT=xcodes[:, 128 * m : 128 * m + 128].bitcast(E4),
                lhsT_scale=xscales[:, 128 * m : 128 * m + 128],
                rhs=tcodes[i][:].bitcast(E5),
                rhs_scale=tscales[i][:],
                start=True,
                stop=True,
            )
            dw_bank[(i, m)] = bank

        def dw_out(i, m, on_vector):
            r, k = m % 4, m // 4
            if r == 0:
                stages["dw"] = stage.tile([P, 4, 512], F32, name="stage", tag="stage")
            st = stages["dw"]
            copy(
                on_vector,
                st[:, r, :].rearrange("p (m t) -> p m t", t=4),
                dw_bank[(i, m)][:].rearrange("p (t m) -> p m t", t=4),
            )
            if r == 3:
                col, out = chunks[i][3], chunks[i][4]
                nc.gpsimd.dma_start(
                    out=out[512 * k : 512 * k + 512, col : col + 512].rearrange("(q r) f -> q r f", r=4),
                    in_=st[:],
                )

        nc.sync.dma_start(out=ang[:], in_=angles.rearrange("(p j) i -> p (j i)", j=4))
        load_g(0)
        load_x(0)
        load_x(1)
        load_x(2)
        load_g(1)
        load_w(0, 0)
        load_w(0, 1)
        load_g(2)
        load_w(0, 2)
        late_loads = {
            1: [lambda: load_w(0, 3), lambda: load_g(3)],
            2: [lambda: load_w(1, 0), lambda: load_w(1, 1), lambda: load_g(4), lambda: load_w(1, 2)],
            3: [lambda: load_g(5), lambda: load_w(1, 3), lambda: load_w(2, 0)],
            4: [lambda: load_w(2, 1), lambda: load_w(2, 2)],
            5: [lambda: load_w(2, 3)],
        }

        by_s = ang[:].rearrange("p (a s) -> p s a", s=2)
        nc.scalar.activation(sin_t[:], by_s, ACT.Sin)
        nc.scalar.activation(half_t[:], by_s, ACT.Sin, scale=0.5)
        dv_group()
        x_group(0, True)
        x_group(1, False)
        t_quant(0)
        x_quant(0)
        nc.vector.tensor_tensor(out=sq_t[:], in0=half_t[:], in1=half_t[:], op=ALU.mult)
        nc.vector.tensor_scalar(out=cos_t[:], in0=sq_t[:], scalar1=-2.0, scalar2=1.0, op0=ALU.mult, op1=ALU.add)

        dw_list = [(i, m) for i in range(NCH) for m in range(12)]
        dw_at = [0]

        def dw(count, on_vector=(False, False)):
            pair = dw_list[dw_at[0] : dw_at[0] + count]
            dw_at[0] += count
            for i, m in pair:
                dw_mm(i, m)
            return [lambda i=i, m=m, v=v: dw_out(i, m, v) for (i, m), v in zip(pair, on_vector)]

        def run(items):
            for f in items:
                f()

        w_in_slot = {
            1: [(0, 0), (0, 1)],
            2: [(0, 2), (0, 3), (0, 4)],
            3: [(0, 5), (1, 0), (1, 1)],
            4: [(1, 2), (1, 3), (1, 4)],
            5: [(1, 5), (2, 0), (2, 1)],
        }
        dw_in_slot = {1: 10, 2: 8, 3: 6, 4: 6, 5: 6}
        pending = []

        def w_quant_next():
            if pending:
                w_quant(*pending.pop(0))

        for i in range(1, NCH):
            run(late_loads[i])
            dz_tile(i)
            left = dw_in_slot[i]
            units = list(w_in_slot[i])
            rope_mul(i, 0, 0)
            if i > 1:
                t_quant(i - 1)
            else:
                x_quant(1)
            rope_mul(i, 0, 1)
            if i == 1:
                x_group(2, True)
            w_quant_next()
            d_turn(i - 1, 0)
            d_turn(i - 1, 1)
            d_copy(i - 1, 0, False)
            outs = dw(2)
            d_copy(i - 1, 1, False)
            run(outs)
            left -= 2
            rope_mul(i, 1, 0)
            if i == 1:
                x_quant(2)
            rope_add(i, 0)
            for step in range(3):
                if units:
                    n, w = units.pop(0)
                    w_turn(n, w, 0)
                    w_turn(n, w, 1)
                    if step == 0 and i >= 2:
                        acc_pass(0, i - 2)
                    count = min(2, left)
                    outs = dw(count)
                    left -= count
                    w_copy(n, w, 0, False)
                    w_copy(n, w, 1, False)
                    run(outs)
                    pending.append((n, w))
                if step == 0:
                    rope_mul(i, 1, 1)
                    rope_add(i, 1)
                    f_quant(i - 1)
                if step == 1:
                    rope_add(i, 2)
                    w_quant_next()
                    rope_add(i, 3)
                    w_quant_next()
            while left > 0:
                run(dw(2))
                left -= 2

        t_quant(5)
        d_turn(5, 0)
        d_turn(5, 1)
        outs = dw(2)
        w_quant_next()
        d_copy(5, 0, False)
        d_copy(5, 1, True)
        run(outs)
        tail_units = [(2, 2), (2, 3), (2, 4), (2, 5)]
        for k, (n, w) in enumerate(tail_units):
            w_turn(n, w, 0)
            w_turn(n, w, 1)
            if k == 0:
                acc_pass(0, 4)
            if k == 1:
                f_quant(5)
            outs = dw(2, (False, True))
            w_copy(n, w, 0, False)
            w_copy(n, w, 1, True)
            run(outs)
            pending.append((n, w))
            if k == 1:
                acc_pass(0, 5)
            if k == 2:
                for j in range(4):
                    acc_out(0, j, j % 2 == 1)
            w_quant_next()
        while pending:
            w_quant_next()
        for k in range(8):
            n, j = 1 + k // 4, k % 4
            for i in range(NCH):
                acc_pass(n, i, (j,))
                if i % 2 == 1:
                    run(dw(min(1, len(dw_list) - dw_at[0]), (dw_at[0] % 2 == 1,)))
            acc_out(n, j, k % 2 == 1)
        while dw_at[0] < len(dw_list):
            run(dw(2, (False, True)))
